import numpy as np
import ml_dtypes


def mxq(x, axis, fmt="e4m3"):
    dtype, down = {"e4m3": (ml_dtypes.float8_e4m3fn, 7), "e5m2": (ml_dtypes.float8_e5m2, 14)}[fmt]
    v = np.moveaxis(np.asarray(x, np.float32).astype(ml_dtypes.bfloat16).astype(np.float64), axis, -1)
    blocks = v.reshape(v.shape[:-1] + (-1, 32))
    amax = np.abs(blocks).max(-1, keepdims=True)
    byte = np.maximum(np.where(amax > 0, np.frexp(amax)[1] - 1 + 127, 0) - down, 1)
    scale = np.exp2(byte - 127.0)
    codes = (blocks / scale).astype(np.float32).astype(dtype).astype(np.float64)
    return np.moveaxis((codes * scale).reshape(v.shape), -1, axis)


WIDE = False


def mx_kscale(k):
    if not WIDE:
        return np.ones(k)
    levels = np.array([10, -10, 5, -5, 0])
    if k % 512:
        return np.exp2(np.random.permutation(np.resize(levels, k // 32))).repeat(32)
    a = np.empty((k // 512, 16))
    for p in range(k // 512):
        a[p, :8] = np.random.permutation(np.resize(levels, 8))
        for g in range(8):
            far = levels[np.abs(levels - a[p, g]) >= 10]
            a[p, g + 8] = far[np.random.randint(len(far))]
    return np.exp2(a.ravel()).repeat(32)


BF16 = ml_dtypes.bfloat16


def bf(x):
    return np.asarray(x, np.float32).astype(BF16)


def f64(x):
    return np.asarray(x).astype(np.float64)


B, H, W, C = 128, 7, 7, 512
G = C // 4
NBR = 3


def setup_inputs():
    s = mx_kscale(C)
    return {
        "h_mix": bf(0.8 * np.random.standard_normal((B, H, W, C)) * s),
        "w_mix": bf(0.8 * np.random.standard_normal((B, H, W, C)) * s),
        "c_proj": bf(np.random.standard_normal((B, H, W, C)) * s),
        "gate_hid": bf(0.6 * np.random.standard_normal((B, G))),
        "wa2": bf(2.0 * np.random.standard_normal((G, C * NBR)) / np.sqrt(G)),
        "ba2": bf(0.6 * np.random.standard_normal(C * NBR)),
        "wo": bf(np.random.standard_normal((C, C)) / np.sqrt(C) / s[:, None]),
        "bo": bf(0.3 * np.random.standard_normal(C)),
    }


def reference(h_mix, w_mix, c_proj, gate_hid, wa2, ba2, wo, bo):
    z = f64(gate_hid) @ f64(wa2) + f64(ba2)
    z = z.reshape(B, C, NBR).transpose(2, 0, 1)
    e = np.exp(z - z.max(0, keepdims=True))
    a = (e / e.sum(0, keepdims=True))[:, :, None, None, :]
    fused = f64(h_mix) * a[0] + f64(w_mix) * a[1] + f64(c_proj) * a[2]
    return (mxq(fused, 3, "e4m3") @ mxq(f64(wo), 0, "e4m3")) + f64(bo)

@@ -1,0 +1,268 @@
+from contextlib import ExitStack
+
+import concourse.mybir as mybir
+from concourse.masks import make_identity
+
+FLOPS = 2 * 128 * 49 * 512 * 512 + 2 * 128 * 128 * 1536
+
+F32 = mybir.dt.float32
+BF16 = mybir.dt.bfloat16
+I32 = mybir.dt.int32
+U32 = mybir.dt.uint32
+U8 = mybir.dt.uint8
+FP8X4 = mybir.dt.float8_e4m3fn_x4
+ALU = mybir.AluOpType
+ACT = mybir.ActivationFunctionType
+
+P = 128
+C = 512
+PACK = 4
+STREAMS = 3
+POSITIONS = 49
+GROUP = 2
+BATCH = 4
+CHUNK = 8
+
+
+def tile_hiremodule_pc_t_kernel(tc, h_mix, w_mix, c_proj, gate_hid, wa2, ba2, wo, bo, out):
+    nc = tc.nc
+    streams = [x.rearrange("b i j c -> b (i j) c") for x in (h_mix, w_mix, c_proj)]
+    out_rows = out.rearrange("b i j c -> b (i j) c")
+
+    n_chunks = (POSITIONS + CHUNK - 1) // CHUNK
+    n_batches = (POSITIONS + BATCH - 1) // BATCH
+    n_groups = (POSITIONS + GROUP - 1) // GROUP
+
+    def span(index, size):
+        return index * size, min(size, POSITIONS - index * size)
+
+    def w_on_gpsimd(first):
+        return (first // BATCH) % 3 == 2
+
+    with ExitStack() as ctx:
+        ctx.enter_context(tc.manual_schedule())
+        const = ctx.enter_context(tc.tile_pool(name="const", bufs=1))
+        x_pool = ctx.enter_context(tc.tile_pool(name="x", bufs=4))
+        prod_pool = ctx.enter_context(tc.tile_pool(name="prod", bufs=3))
+        quant_pool = ctx.enter_context(tc.tile_pool(name="quant", bufs=3))
+        out_pool = ctx.enter_context(tc.tile_pool(name="outs", bufs=4))
+        psum_gate = ctx.enter_context(tc.psum_pool(name="psum_gate", bufs=1))
+        psum_sum = ctx.enter_context(tc.psum_pool(name="psum_sum", bufs=4))
+        psum_out = ctx.enter_context(tc.psum_pool(name="psum_out", bufs=2))
+
+        bias_rows = const.tile([P, STREAMS * C + C], BF16, name="bias_rows")
+        ones = const.tile([P, P], BF16, name="ones")
+        warm = const.tile([P, 2], F32, name="warm")
+        ident_bf16 = const.tile([P, P], BF16, name="ident_bf16")
+        ident_f32 = const.tile([P, P], F32, name="ident_f32")
+        gate_sb = const.tile([P, P], BF16, name="gate_sb")
+        gate_t = const.tile([P, P], BF16, name="gate_t")
+        wa2_sb = const.tile([P, STREAMS * C], BF16, name="wa2_sb")
+        wo_rows = const.tile([P, PACK, C], BF16, name="wo_rows")
+        wo_grouped = const.tile([P, C, PACK], BF16, name="wo_grouped", align_bytes=64)
+        wo_codes = const.tile([P, C], U32, name="wo_codes", align_bytes=64)
+        wo_scales = const.tile([P, C], U8, name="wo_scales", align_bytes=64)
+        bo_all = const.tile([P, C], F32, name="bo_all")
+        gate = [const.tile([P, C], F32, name="gate%d" % k) for k in range(STREAMS)]
+        top = const.tile([P, C], F32, name="top")
+        total = const.tile([P, C], F32, name="total")
+        gate_flipped = [const.tile([P, PACK, P], F32, name="gate_flipped%d" % k) for k in range(2)]
+
+        nc.vector.memset(bias_rows[:].bitcast(I32), 0)
+        nc.vector.memset(ones[:], 1.0)
+        nc.vector.memset(warm[:, 0:1], 0.0)
+        nc.scalar.activation(out=warm[:, 1:2], in_=warm[:, 0:1], func=ACT.Exp)
+        make_identity(nc, ident_bf16[:])
+        make_identity(nc, ident_f32[:])
+
+        nc.sync.dma_start(out=gate_sb[:], in_=gate_hid)
+        nc.sync.dma_start(out=bias_rows[0:1, 0 : STREAMS * C], in_=ba2.unsqueeze(0))
+        nc.sync.dma_start(out=wa2_sb[:], in_=wa2)
+        nc.sync.dma_start(out=bias_rows[0:1, STREAMS * C :], in_=bo.unsqueeze(0))
+        nc.sync.dma_start(out=wo_rows[:], in_=wo.rearrange("(p t) n -> p t n", t=PACK))
+
+        x_tiles = {}
+
+        def load_chunk(chunk):
+            first, n = span(chunk, CHUNK)
+            for k in range(STREAMS):
+                x = x_pool.tile([P, n, C], BF16, name="x%d_%d" % (k, chunk), tag="x%d" % k)
+                nc.sync.dma_start(out=x[:], in_=streams[k][:, first : first + n, :])
+                x_tiles[(k, chunk)] = x
+
+        for chunk in range(4):
+            load_chunk(chunk)
+
+        nc.gpsimd.tensor_scalar(
+            out=wo_grouped[:],
+            in0=wo_rows[:].rearrange("p t n -> p n t"),
+            scalar1=1.0,
+            scalar2=0.0,
+            op0=ALU.mult,
+            op1=ALU.add,
+        )
+
+        flipped = psum_out.tile([P, P], BF16, name="flipped", tag="o")
+        nc.tensor.transpose(flipped[:], gate_sb[:], ident_bf16[:])
+        nc.vector.tensor_copy(out=gate_t[:], in_=flipped[:])
+
+        ba2_by_stream = bias_rows[:, 0 : STREAMS * C].rearrange("g (q t k) -> g k t q", t=PACK, k=STREAMS)
+        wa2_by_stream = wa2_sb[:].rearrange("g (q t k) -> g k t q", t=PACK, k=STREAMS)
+        z = [psum_sum.tile([P, C], F32, name="z%d" % k, tag="f") for k in range(STREAMS)]
+        for k in range(STREAMS):
+            nc.tensor.matmul(z[k][:], lhsT=ones[:], rhs=ba2_by_stream[:, k, :, :], start=True, stop=False)
+        bo_psum = psum_out.tile([P, C], F32, name="bo_psum", tag="o")
+        nc.tensor.matmul(bo_psum[:], lhsT=ones[:], rhs=bias_rows[:, STREAMS * C :], start=True, stop=True)
+        for k in range(STREAMS):
+            nc.tensor.matmul(z[k][:], lhsT=gate_t[:], rhs=wa2_by_stream[:, k, :, :], start=False, stop=True)
+
+        nc.scalar.copy(out=gate[0][:], in_=z[0][:])
+        nc.vector.tensor_tensor(out=top[:], in0=z[1][:], in1=gate[0][:], op=ALU.max)
+        nc.vector.tensor_tensor(out=top[:], in0=z[2][:], in1=top[:], op=ALU.max)
+        nc.vector.tensor_tensor(out=gate[2][:], in0=z[2][:], in1=top[:], op=ALU.subtract)
+        nc.scalar.activation(out=gate[2][:], in_=gate[2][:], func=ACT.Exp)
+        nc.vector.tensor_tensor(out=gate[0][:], in0=gate[0][:], in1=top[:], op=ALU.subtract)
+        nc.scalar.activation(out=gate[0][:], in_=gate[0][:], func=ACT.Exp)
+        nc.vector.tensor_tensor(out=gate[1][:], in0=z[1][:], in1=top[:], op=ALU.subtract)
+        nc.scalar.activation(out=gate[1][:], in_=gate[1][:], func=ACT.Exp)
+        nc.scalar.copy(out=bo_all[:], in_=bo_psum[:])
+        nc.vector.quantize_mx(
+            out=wo_codes[:].bitcast(FP8X4),
+            scales=wo_scales[:],
+            in_=wo_grouped[:].rearrange("p n t -> p (n t)"),
+        )
+        nc.vector.tensor_tensor(out=total[:], in0=gate[2][:], in1=gate[0][:], op=ALU.add)
+        nc.vector.tensor_tensor(out=total[:], in0=total[:], in1=gate[1][:], op=ALU.add)
+        nc.vector.reciprocal(out=total[:], in_=total[:])
+        for k in range(2):
+            nc.vector.tensor_tensor(out=gate[k][:], in0=gate[k][:], in1=total[:], op=ALU.mult)
+
+        gate_psum = [psum_gate.tile([P, C], F32, name="gate_psum%d" % k, tag="a%d" % k) for k in range(2)]
+        for k in range(2):
+            turned = psum_sum.tile([P, PACK, P], F32, name="turned%d" % k, tag="f")
+            for t in range(PACK):
+                nc.tensor.transpose(turned[:, t, :], gate[k][:, t * P : (t + 1) * P], ident_f32[:])
+            nc.scalar.copy(out=gate_flipped[k][:], in_=turned[:])
+        for k in range(2):
+            for t in range(PACK):
+                nc.tensor.transpose(gate_psum[k][:, t * P : (t + 1) * P], gate_flipped[k][:, t, :], ident_f32[:])
+
+        products = {}
+        grouped_tiles = {}
+        code_tiles = {}
+        out_banks = {}
+        out_tiles = {}
+
+        def multiply(engine, k, group, a_k, tag, bufs):
+            first, n = span(group, GROUP)
+            chunk = first // CHUNK
+            product = prod_pool.tile([P, n, C], F32, name="%s_%d" % (tag, group), tag=tag, bufs=bufs)
+            engine.tensor_tensor(
+                out=product[:].rearrange("b j (t q) -> b j t q", t=PACK),
+                in0=x_tiles[(k, chunk)][:, first % CHUNK : first % CHUNK + n, :].rearrange(
+                    "b j (q t) -> b j t q", t=PACK
+                ),
+                in1=a_k[:].rearrange("b (t q) -> b t q", t=PACK).unsqueeze(1).to_broadcast([P, n, PACK, P]),
+                op=ALU.mult,
+            )
+            for j in range(n):
+                products[(k, first + j)] = (product, j)
+
+        def vector_products(group, a):
+            multiply(nc.vector, 0, group, a[0], "vector0", 3)
+            if not w_on_gpsimd(group * GROUP):
+                multiply(nc.vector, 1, group, a[1], "vector1", 3)
+
+        def gpsimd_products(group):
+            if w_on_gpsimd(group * GROUP):
+                multiply(nc.gpsimd, 1, group, gate[1], "gpsimd1", 3)
+            multiply(nc.gpsimd, 2, group, gate[2], "gpsimd2", 4)
+
+        def sum_transposed(group):
+            first, n = span(group, GROUP)
+            batch = first // BATCH
+            if first % BATCH == 0:
+                grouped_tiles[batch] = quant_pool.tile(
+                    [P, BATCH, P, PACK], BF16, name="grouped%d" % batch, tag="grouped", align_bytes=64
+                )
+            sums = [psum_sum.tile([P, PACK, P], F32, name="sum%d" % (first + j), tag="f") for j in range(n)]
+            for k in range(STREAMS):
+                for j in range(n):
+                    product, index = products[(k, first + j)]
+                    for t in range(PACK):
+                        nc.tensor.matmul(
+                            sums[j][:, t, :],
+                            lhsT=product[:, index, t * P : (t + 1) * P],
+                            rhs=ident_f32[:],
+                            is_transpose=True,
+                            start=(k == 0 and t == 0),
+                            stop=(k == STREAMS - 1 and t == PACK - 1),
+                        )
+            for j in range(n):
+                nc.scalar.copy(
+                    out=grouped_tiles[batch][:, first % BATCH + j, :, :],
+                    in_=sums[j][:].rearrange("p t b -> p b t"),
+                )
+
+        def quantise(batch):
+            n = span(batch, BATCH)[1]
+            codes = quant_pool.tile([P, BATCH * P], U32, name="codes%d" % batch, tag="codes", align_bytes=64)
+            scales = quant_pool.tile([P, BATCH * P], U8, name="scales%d" % batch, tag="scales", align_bytes=64)
+            code_tiles[batch] = (codes, scales)
+            nc.vector.quantize_mx(
+                out=codes[:, 0 : n * P].bitcast(FP8X4),
+                scales=scales[:, 0 : n * P],
+                in_=grouped_tiles[batch][:, 0:n, :, :].rearrange("p j b t -> p (j b t)"),
+            )
+
+        def project(group):
+            first, n = span(group, GROUP)
+            codes, scales = code_tiles[first // BATCH]
+            for position in range(first, first + n):
+                columns = slice((position % BATCH) * P, (position % BATCH + 1) * P)
+                bank = psum_out.tile([P, C], F32, name="bank%d" % position, tag="o")
+                nc.tensor.matmul_mx(
+                    out=bank[:],
+                    lhsT=codes[:, columns].bitcast(FP8X4),
+                    lhsT_scale=scales[:, columns],
+                    rhs=wo_codes[:].bitcast(FP8X4),
+                    rhs_scale=wo_scales[:],
+                    start=True,
+                    stop=True,
+                )
+                out_banks[position] = bank
+
+        def add_bias(group):
+            first, n = span(group, GROUP)
+            out_tiles[group] = out_pool.tile([P, GROUP, C], F32, name="out%d" % group, tag="out")
+            for j in range(n):
+                nc.vector.tensor_tensor(
+                    out=out_tiles[group][:, j, :], in0=out_banks[first + j][:], in1=bo_all[:], op=ALU.add
+                )
+
+        def store(group):
+            first, n = span(group, GROUP)
+            nc.scalar.dma_start(out=out_rows[:, first : first + n, :], in_=out_tiles[group][:, 0:n, :])
+
+        vector_products(0, gate)
+        nc.vector.tensor_tensor(out=gate[2][:], in0=gate[2][:], in1=total[:], op=ALU.mult)
+        gpsimd_products(0)
+        gpsimd_products(1)
+
+        for step in range(n_groups + 5):
+            if step % 2 == 0 and 0 <= step // 2 - 2 < n_batches:
+                quantise(step // 2 - 2)
+            if 0 <= step - 5 < n_groups:
+                add_bias(step - 5)
+            if 1 <= step < n_groups:
+                vector_products(step, gate_psum)
+            if step + 2 < n_groups:
+                gpsimd_products(step + 2)
+            if step % 4 == 3 and step // 4 + 4 < n_chunks:
+                load_chunk(step // 4 + 4)
+            if 0 <= step - 1 < n_groups:
+                sum_transposed(step - 1)
+            if 0 <= step - 4 < n_groups:
+                project(step - 4)
+            if 0 <= step - 5 < n_groups:
+                store(step - 5)

@@ -17,6 +17,8 @@ ACT = mybir.ActivationFunctionType
 P = 128
 C = 512
 PACK = 4
+RUN = 8
+BLOCKS = C // (PACK * RUN)
 STREAMS = 3
 POSITIONS = 49
 GROUP = 2
@@ -79,7 +81,11 @@ def tile_hiremodule_pc_t_kernel(tc, h_mix, w_mix, c_proj, gate_hid, wa2, ba2, wo
         nc.sync.dma_start(out=bias_rows[0:1, 0 : STREAMS * C], in_=ba2.unsqueeze(0))
         nc.sync.dma_start(out=wa2_sb[:], in_=wa2)
         nc.sync.dma_start(out=bias_rows[0:1, STREAMS * C :], in_=bo.unsqueeze(0))
-        nc.sync.dma_start(out=wo_rows[:], in_=wo.rearrange("(p t) n -> p t n", t=PACK))
+        for s in range(BLOCKS):
+            nc.sync.dma_start(
+                out=wo_rows[s * RUN : (s + 1) * RUN, :, :],
+                in_=wo[s * PACK * RUN : (s + 1) * PACK * RUN, :].rearrange("(t r) n -> r t n", t=PACK),
+            )
 
         x_tiles = {}
 
@@ -106,15 +112,15 @@ def tile_hiremodule_pc_t_kernel(tc, h_mix, w_mix, c_proj, gate_hid, wa2, ba2, wo
         nc.tensor.transpose(flipped[:], gate_sb[:], ident_bf16[:])
         nc.vector.tensor_copy(out=gate_t[:], in_=flipped[:])
 
-        ba2_by_stream = bias_rows[:, 0 : STREAMS * C].rearrange("g (q t k) -> g k t q", t=PACK, k=STREAMS)
-        wa2_by_stream = wa2_sb[:].rearrange("g (q t k) -> g k t q", t=PACK, k=STREAMS)
+        ba2_by_stream = bias_rows[:, 0 : STREAMS * C].rearrange("g (s t r k) -> g k t s r", t=PACK, r=RUN, k=STREAMS)
+        wa2_by_stream = wa2_sb[:].rearrange("g (s t r k) -> g k t s r", t=PACK, r=RUN, k=STREAMS)
         z = [psum_sum.tile([P, C], F32, name="z%d" % k, tag="f") for k in range(STREAMS)]
         for k in range(STREAMS):
-            nc.tensor.matmul(z[k][:], lhsT=ones[:], rhs=ba2_by_stream[:, k, :, :], start=True, stop=False)
+            nc.tensor.matmul(z[k][:], lhsT=ones[:], rhs=ba2_by_stream[:, k, :, :, :], start=True, stop=False)
         bo_psum = psum_out.tile([P, C], F32, name="bo_psum", tag="o")
         nc.tensor.matmul(bo_psum[:], lhsT=ones[:], rhs=bias_rows[:, STREAMS * C :], start=True, stop=True)
         for k in range(STREAMS):
-            nc.tensor.matmul(z[k][:], lhsT=gate_t[:], rhs=wa2_by_stream[:, k, :, :], start=False, stop=True)
+            nc.tensor.matmul(z[k][:], lhsT=gate_t[:], rhs=wa2_by_stream[:, k, :, :, :], start=False, stop=True)
 
         nc.scalar.copy(out=gate[0][:], in_=z[0][:])
         nc.vector.tensor_tensor(out=top[:], in0=z[1][:], in1=gate[0][:], op=ALU.max)
@@ -156,13 +162,16 @@ def tile_hiremodule_pc_t_kernel(tc, h_mix, w_mix, c_proj, gate_hid, wa2, ba2, wo
         def multiply(engine, k, group, a_k, tag, bufs):
             first, n = span(group, GROUP)
             chunk = first // CHUNK
-            product = prod_pool.tile([P, n, C], F32, name="%s_%d" % (tag, group), tag=tag, bufs=bufs)
+            product = prod_pool.tile([P, PACK, n, P], F32, name="%s_%d" % (tag, group), tag=tag, bufs=bufs)
             engine.tensor_tensor(
-                out=product[:].rearrange("b j (t q) -> b j t q", t=PACK),
+                out=product[:].rearrange("b t j (s r) -> b t j s r", r=RUN),
                 in0=x_tiles[(k, chunk)][:, first % CHUNK : first % CHUNK + n, :].rearrange(
-                    "b j (q t) -> b j t q", t=PACK
+                    "b j (s t r) -> b t j s r", t=PACK, r=RUN
                 ),
-                in1=a_k[:].rearrange("b (t q) -> b t q", t=PACK).unsqueeze(1).to_broadcast([P, n, PACK, P]),
+                in1=a_k[:]
+                .rearrange("b (t s r) -> b t s r", t=PACK, r=RUN)
+                .unsqueeze(2)
+                .to_broadcast([P, PACK, n, BLOCKS, RUN]),
                 op=ALU.mult,
             )
             for j in range(n):
@@ -192,7 +201,7 @@ def tile_hiremodule_pc_t_kernel(tc, h_mix, w_mix, c_proj, gate_hid, wa2, ba2, wo
                     for t in range(PACK):
                         nc.tensor.matmul(
                             sums[j][:, t, :],
-                            lhsT=product[:, index, t * P : (t + 1) * P],
+                            lhsT=product[:, t, index, :],
                             rhs=ident_f32[:],
                             is_transpose=True,
                             start=(k == 0 and t == 0),

@@ -24,6 +24,7 @@ POSITIONS = 49
 GROUP = 2
 BATCH = 4
 CHUNK = 8
+WARM_MATMULS = 12
 
 
 def tile_hiremodule_pc_t_kernel(tc, h_mix, w_mix, c_proj, gate_hid, wa2, ba2, wo, bo, out):
@@ -38,8 +39,11 @@ def tile_hiremodule_pc_t_kernel(tc, h_mix, w_mix, c_proj, gate_hid, wa2, ba2, wo
     def span(index, size):
         return index * size, min(size, POSITIONS - index * size)
 
-    def w_on_gpsimd(first):
-        return (first // BATCH) % 3 == 2
+    def w_on_gpsimd(group):
+        return group % 6 == 5 and group >= 11
+
+    def is_flipped(batch):
+        return batch % 2 == 0 and batch < 9
 
     with ExitStack() as ctx:
         ctx.enter_context(tc.manual_schedule())
@@ -54,32 +58,43 @@ def tile_hiremodule_pc_t_kernel(tc, h_mix, w_mix, c_proj, gate_hid, wa2, ba2, wo
 
         bias_rows = const.tile([P, STREAMS * C + C], BF16, name="bias_rows")
         ones = const.tile([P, P], BF16, name="ones")
+        pick = [const.tile([P, P], BF16, name="pick%d" % k) for k in (1, 2)]
         warm = const.tile([P, 2], F32, name="warm")
         ident_bf16 = const.tile([P, P], BF16, name="ident_bf16")
         ident_f32 = const.tile([P, P], F32, name="ident_f32")
         gate_sb = const.tile([P, P], BF16, name="gate_sb")
         gate_t = const.tile([P, P], BF16, name="gate_t")
+        minus_gate_t = const.tile([P, P], BF16, name="minus_gate_t")
         wa2_sb = const.tile([P, STREAMS * C], BF16, name="wa2_sb")
         wo_rows = const.tile([P, PACK, C], BF16, name="wo_rows")
         wo_grouped = const.tile([P, C, PACK], BF16, name="wo_grouped", align_bytes=64)
         wo_codes = const.tile([P, C], U32, name="wo_codes", align_bytes=64)
         wo_scales = const.tile([P, C], U8, name="wo_scales", align_bytes=64)
         bo_all = const.tile([P, C], F32, name="bo_all")
+        bo_column = const.tile([P, PACK, 1], F32, name="bo_column")
         gate = [const.tile([P, C], F32, name="gate%d" % k) for k in range(STREAMS)]
         top = const.tile([P, C], F32, name="top")
         total = const.tile([P, C], F32, name="total")
         gate_flipped = [const.tile([P, PACK, P], F32, name="gate_flipped%d" % k) for k in range(2)]
 
-        nc.vector.memset(bias_rows[:].bitcast(I32), 0)
         nc.vector.memset(ones[:], 1.0)
+        nc.gpsimd.memset(bias_rows[:].bitcast(I32), 0)
+        for k in (1, 2):
+            nc.vector.memset(pick[k - 1][:].bitcast(I32), 0)
+            nc.vector.memset(pick[k - 1][0:1, :], -1.0)
+            nc.vector.memset(pick[k - 1][32 * k : 32 * k + 1, :], 1.0)
         nc.vector.memset(warm[:, 0:1], 0.0)
         nc.scalar.activation(out=warm[:, 1:2], in_=warm[:, 0:1], func=ACT.Exp)
         make_identity(nc, ident_bf16[:])
         make_identity(nc, ident_f32[:])
 
         nc.sync.dma_start(out=gate_sb[:], in_=gate_hid)
-        nc.sync.dma_start(out=bias_rows[0:1, 0 : STREAMS * C], in_=ba2.unsqueeze(0))
         nc.sync.dma_start(out=wa2_sb[:], in_=wa2)
+        for k in range(STREAMS):
+            nc.sync.dma_start(
+                out=bias_rows[32 * k : 32 * k + 1, 0 : STREAMS * C - 2],
+                in_=ba2.unsqueeze(0)[:, k : STREAMS * C - 2 + k],
+            )
         nc.sync.dma_start(out=bias_rows[0:1, STREAMS * C :], in_=bo.unsqueeze(0))
         for s in range(BLOCKS):
             nc.sync.dma_start(
@@ -108,40 +123,40 @@ def tile_hiremodule_pc_t_kernel(tc, h_mix, w_mix, c_proj, gate_hid, wa2, ba2, wo
             op1=ALU.add,
         )
 
+        spare = psum_out.tile([P, C], F32, name="spare", tag="o")
+        for i in range(WARM_MATMULS):
+            nc.tensor.matmul(spare[:, 0:P], lhsT=ones[:], rhs=ones[:], start=True, stop=True)
+
         flipped = psum_out.tile([P, P], BF16, name="flipped", tag="o")
         nc.tensor.transpose(flipped[:], gate_sb[:], ident_bf16[:])
         nc.vector.tensor_copy(out=gate_t[:], in_=flipped[:])
+        nc.scalar.mul(out=minus_gate_t[:], in_=flipped[:], mul=-1.0)
 
         ba2_by_stream = bias_rows[:, 0 : STREAMS * C].rearrange("g (s t r k) -> g k t s r", t=PACK, r=RUN, k=STREAMS)
         wa2_by_stream = wa2_sb[:].rearrange("g (s t r k) -> g k t s r", t=PACK, r=RUN, k=STREAMS)
-        z = [psum_sum.tile([P, C], F32, name="z%d" % k, tag="f") for k in range(STREAMS)]
-        for k in range(STREAMS):
-            nc.tensor.matmul(z[k][:], lhsT=ones[:], rhs=ba2_by_stream[:, k, :, :, :], start=True, stop=False)
+        diff = {k: psum_sum.tile([P, C], F32, name="diff%d" % k, tag="f") for k in (1, 2)}
+        for k in (1, 2):
+            nc.tensor.matmul(diff[k][:], lhsT=gate_t[:], rhs=wa2_by_stream[:, k, :, :, :], start=True, stop=False)
+            nc.tensor.matmul(diff[k][:], lhsT=minus_gate_t[:], rhs=wa2_by_stream[:, 0, :, :, :], start=False, stop=False)
+            nc.tensor.matmul(diff[k][:], lhsT=pick[k - 1][:], rhs=ba2_by_stream[:, 0, :, :, :], start=False, stop=True)
         bo_psum = psum_out.tile([P, C], F32, name="bo_psum", tag="o")
         nc.tensor.matmul(bo_psum[:], lhsT=ones[:], rhs=bias_rows[:, STREAMS * C :], start=True, stop=True)
-        for k in range(STREAMS):
-            nc.tensor.matmul(z[k][:], lhsT=gate_t[:], rhs=wa2_by_stream[:, k, :, :, :], start=False, stop=True)
 
-        nc.scalar.copy(out=gate[0][:], in_=z[0][:])
-        nc.vector.tensor_tensor(out=top[:], in0=z[1][:], in1=gate[0][:], op=ALU.max)
-        nc.vector.tensor_tensor(out=top[:], in0=z[2][:], in1=top[:], op=ALU.max)
-        nc.vector.tensor_tensor(out=gate[2][:], in0=z[2][:], in1=top[:], op=ALU.subtract)
-        nc.scalar.activation(out=gate[2][:], in_=gate[2][:], func=ACT.Exp)
-        nc.vector.tensor_tensor(out=gate[0][:], in0=gate[0][:], in1=top[:], op=ALU.subtract)
-        nc.scalar.activation(out=gate[0][:], in_=gate[0][:], func=ACT.Exp)
-        nc.vector.tensor_tensor(out=gate[1][:], in0=z[1][:], in1=top[:], op=ALU.subtract)
-        nc.scalar.activation(out=gate[1][:], in_=gate[1][:], func=ACT.Exp)
-        nc.scalar.copy(out=bo_all[:], in_=bo_psum[:])
-        nc.vector.quantize_mx(
-            out=wo_codes[:].bitcast(FP8X4),
-            scales=wo_scales[:],
-            in_=wo_grouped[:].rearrange("p n t -> p (n t)"),
+        nc.scalar.copy(out=gate[1][:], in_=diff[1][:])
+        nc.vector.scalar_tensor_tensor(
+            out=top[:], in0=diff[2][:], scalar=0.0, in1=gate[1][:], op0=ALU.max, op1=ALU.max
         )
+        nc.scalar.activation(out=gate[0][:], in_=top[:], func=ACT.Exp, scale=-1.0)
+        nc.vector.tensor_tensor(out=gate[2][:], in0=diff[2][:], in1=top[:], op=ALU.subtract)
+        nc.scalar.activation(out=gate[2][:], in_=gate[2][:], func=ACT.Exp)
+        nc.vector.tensor_tensor(out=gate[1][:], in0=diff[1][:], in1=top[:], op=ALU.subtract)
+        nc.scalar.activation(out=gate[1][:], in_=gate[1][:], func=ACT.Exp)
         nc.vector.tensor_tensor(out=total[:], in0=gate[2][:], in1=gate[0][:], op=ALU.add)
         nc.vector.tensor_tensor(out=total[:], in0=total[:], in1=gate[1][:], op=ALU.add)
         nc.vector.reciprocal(out=total[:], in_=total[:])
-        for k in range(2):
+        for k in (2, 0, 1):
             nc.vector.tensor_tensor(out=gate[k][:], in0=gate[k][:], in1=total[:], op=ALU.mult)
+        nc.scalar.copy(out=bo_all[:], in_=bo_psum[:])
 
         gate_psum = [psum_gate.tile([P, C], F32, name="gate_psum%d" % k, tag="a%d" % k) for k in range(2)]
         for k in range(2):
@@ -153,39 +168,47 @@ def tile_hiremodule_pc_t_kernel(tc, h_mix, w_mix, c_proj, gate_hid, wa2, ba2, wo
             for t in range(PACK):
                 nc.tensor.transpose(gate_psum[k][:, t * P : (t + 1) * P], gate_flipped[k][:, t, :], ident_f32[:])
 
+        turned = psum_sum.tile([P, PACK, P], F32, name="turned_bo", tag="f")
+        for c in range(PACK):
+            nc.tensor.transpose(turned[:, c, :], bo_all[:, c * P : (c + 1) * P], ident_f32[:])
+        nc.scalar.copy(out=bo_column[:], in_=turned[:, :, 0:1])
+
         products = {}
         grouped_tiles = {}
         code_tiles = {}
         out_banks = {}
         out_tiles = {}
+        flipped_tiles = {}
 
-        def multiply(engine, k, group, a_k, tag, bufs):
-            first, n = span(group, GROUP)
-            chunk = first // CHUNK
-            product = prod_pool.tile([P, PACK, n, P], F32, name="%s_%d" % (tag, group), tag=tag, bufs=bufs)
-            engine.tensor_tensor(
-                out=product[:].rearrange("b t j (s r) -> b t j s r", r=RUN),
-                in0=x_tiles[(k, chunk)][:, first % CHUNK : first % CHUNK + n, :].rearrange(
-                    "b j (s t r) -> b t j s r", t=PACK, r=RUN
-                ),
-                in1=a_k[:]
-                .rearrange("b (t s r) -> b t s r", t=PACK, r=RUN)
-                .unsqueeze(2)
-                .to_broadcast([P, PACK, n, BLOCKS, RUN]),
-                op=ALU.mult,
-            )
-            for j in range(n):
-                products[(k, first + j)] = (product, j)
+        def multiply(engine, k, group, a_k, tag, bufs, at_once=GROUP):
+            start, count = span(group, GROUP)
+            for first in range(start, start + count, at_once):
+                n = min(at_once, start + count - first)
+                chunk = first // CHUNK
+                product = prod_pool.tile([P, PACK, n, P], F32, name="%s_%d" % (tag, first), tag=tag, bufs=bufs * GROUP // at_once)
+                engine.tensor_tensor(
+                    out=product[:].rearrange("b t j (s r) -> b t j s r", r=RUN),
+                    in0=x_tiles[(k, chunk)][:, first % CHUNK : first % CHUNK + n, :].rearrange(
+                        "b j (s t r) -> b t j s r", t=PACK, r=RUN
+                    ),
+                    in1=a_k[:]
+                    .rearrange("b (t s r) -> b t s r", t=PACK, r=RUN)
+                    .unsqueeze(2)
+                    .to_broadcast([P, PACK, n, BLOCKS, RUN]),
+                    op=ALU.mult,
+                )
+                for j in range(n):
+                    products[(k, first + j)] = (product, j)
 
         def vector_products(group, a):
             multiply(nc.vector, 0, group, a[0], "vector0", 3)
-            if not w_on_gpsimd(group * GROUP):
+            if not w_on_gpsimd(group):
                 multiply(nc.vector, 1, group, a[1], "vector1", 3)
 
         def gpsimd_products(group):
-            if w_on_gpsimd(group * GROUP):
-                multiply(nc.gpsimd, 1, group, gate[1], "gpsimd1", 3)
-            multiply(nc.gpsimd, 2, group, gate[2], "gpsimd2", 4)
+            if w_on_gpsimd(group):
+                multiply(nc.gpsimd, 1, group, gate[1], "gpsimd1", 3, 1)
+            multiply(nc.gpsimd, 2, group, gate[2], "gpsimd2", 4, 1)
 
         def sum_transposed(group):
             first, n = span(group, GROUP)
@@ -224,12 +247,12 @@ def tile_hiremodule_pc_t_kernel(tc, h_mix, w_mix, c_proj, gate_hid, wa2, ba2, wo
                 in_=grouped_tiles[batch][:, 0:n, :, :].rearrange("p j b t -> p (j b t)"),
             )
 
-        def project(group):
+        def project(group, pool=psum_out, tag="o"):
             first, n = span(group, GROUP)
             codes, scales = code_tiles[first // BATCH]
             for position in range(first, first + n):
                 columns = slice((position % BATCH) * P, (position % BATCH + 1) * P)
-                bank = psum_out.tile([P, C], F32, name="bank%d" % position, tag="o")
+                bank = pool.tile([P, C], F32, name="bank%d" % position, tag=tag)
                 nc.tensor.matmul_mx(
                     out=bank[:],
                     lhsT=codes[:, columns].bitcast(FP8X4),
@@ -240,6 +263,40 @@ def tile_hiremodule_pc_t_kernel(tc, h_mix, w_mix, c_proj, gate_hid, wa2, ba2, wo
                     stop=True,
                 )
                 out_banks[position] = bank
+
+        def project_flipped(batch, blocks):
+            codes, scales = code_tiles[batch]
+            if batch not in flipped_tiles:
+                flipped_tiles[batch] = out_pool.tile(
+                    [P, PACK, BATCH * P], F32, name="flipped%d" % batch, tag="flipped", bufs=2
+                )
+            for c in blocks:
+                columns = slice(c * P, (c + 1) * P)
+                bank = psum_out.tile([P, BATCH * P], F32, name="flip%d_%d" % (batch, c), tag="o")
+                nc.tensor.matmul_mx(
+                    out=bank[:],
+                    lhsT=wo_codes[:, columns].bitcast(FP8X4),
+                    lhsT_scale=wo_scales[:, columns],
+                    rhs=codes[:].bitcast(FP8X4),
+                    rhs_scale=scales[:],
+                    start=True,
+                    stop=True,
+                )
+                nc.scalar.activation(
+                    out=flipped_tiles[batch][:, c, :], in_=bank[:], func=ACT.Identity, bias=bo_column[:, c, :]
+                )
+
+        def unflip(group):
+            first, n = span(group, GROUP)
+            out_tiles[group] = out_pool.tile([P, GROUP, C], F32, name="out%d" % group, tag="out")
+            for j in range(n):
+                columns = slice((first % BATCH + j) * P, (first % BATCH + j + 1) * P)
+                bank = psum_sum.tile([P, C], F32, name="unflip%d" % (first + j), tag="f")
+                for c in range(PACK):
+                    nc.tensor.transpose(
+                        bank[:, c * P : (c + 1) * P], flipped_tiles[first // BATCH][:, c, columns], ident_f32[:]
+                    )
+                nc.scalar.copy(out=out_tiles[group][:, j, :], in_=bank[:])
 
         def add_bias(group):
             first, n = span(group, GROUP)
@@ -253,25 +310,50 @@ def tile_hiremodule_pc_t_kernel(tc, h_mix, w_mix, c_proj, gate_hid, wa2, ba2, wo
             first, n = span(group, GROUP)
             nc.scalar.dma_start(out=out_rows[:, first : first + n, :], in_=out_tiles[group][:, 0:n, :])
 
-        vector_products(0, gate)
-        nc.vector.tensor_tensor(out=gate[2][:], in0=gate[2][:], in1=total[:], op=ALU.mult)
         gpsimd_products(0)
         gpsimd_products(1)
+        vector_products(0, gate)
+        nc.vector.quantize_mx(
+            out=wo_codes[:].bitcast(FP8X4),
+            scales=wo_scales[:],
+            in_=wo_grouped[:].rearrange("p n t -> p (n t)"),
+        )
 
-        for step in range(n_groups + 5):
-            if step % 2 == 0 and 0 <= step // 2 - 2 < n_batches:
+        for step in range(n_groups):
+            if step % 2 == 0 and step >= 4:
                 quantise(step // 2 - 2)
-            if 0 <= step - 5 < n_groups:
+            if step >= 5 and not is_flipped((step - 5) // 2):
                 add_bias(step - 5)
-            if 1 <= step < n_groups:
+                store(step - 5)
+            if step >= 1:
                 vector_products(step, gate_psum)
             if step + 2 < n_groups:
                 gpsimd_products(step + 2)
             if step % 4 == 3 and step // 4 + 4 < n_chunks:
                 load_chunk(step // 4 + 4)
-            if 0 <= step - 1 < n_groups:
+            if step >= 1:
                 sum_transposed(step - 1)
-            if 0 <= step - 4 < n_groups:
-                project(step - 4)
-            if 0 <= step - 5 < n_groups:
-                store(step - 5)
+            if step >= 7 and is_flipped((step - 7) // 2):
+                unflip(step - 7)
+                store(step - 7)
+            if step >= 4:
+                if is_flipped((step - 4) // 2):
+                    project_flipped((step - 4) // 2, range(2) if step % 2 == 0 else range(2, PACK))
+                else:
+                    project(step - 4)
+
+        last = n_groups - 1
+        sum_transposed(last)
+        add_bias(last - 4)
+        store(last - 4)
+        quantise(n_batches - 2)
+        project(last - 3)
+        project(last - 2, psum_sum, "f")
+        add_bias(last - 3)
+        store(last - 3)
+        quantise(n_batches - 1)
+        project(last - 1)
+        project(last, psum_sum, "f")
+        for group in range(last - 2, n_groups):
+            add_bias(group)
+            store(group)

@@ -207,8 +207,8 @@ def tile_hiremodule_pc_t_kernel(tc, h_mix, w_mix, c_proj, gate_hid, wa2, ba2, wo
 
         def gpsimd_products(group):
             if w_on_gpsimd(group):
-                multiply(nc.gpsimd, 1, group, gate[1], "gpsimd1", 3, 1)
-            multiply(nc.gpsimd, 2, group, gate[2], "gpsimd2", 4, 1)
+                multiply(nc.gpsimd, 1, group, gate[1], "gpsimd1", 3)
+            multiply(nc.gpsimd, 2, group, gate[2], "gpsimd2", 4)
 
         def sum_transposed(group):
             first, n = span(group, GROUP)

@@ -39,9 +39,6 @@ def tile_hiremodule_pc_t_kernel(tc, h_mix, w_mix, c_proj, gate_hid, wa2, ba2, wo
     def span(index, size):
         return index * size, min(size, POSITIONS - index * size)
 
-    def w_on_gpsimd(group):
-        return group % 6 == 5 and group >= 11
-
     def is_flipped(batch):
         return batch % 2 == 0 and batch < 9
 
@@ -51,7 +48,7 @@ def tile_hiremodule_pc_t_kernel(tc, h_mix, w_mix, c_proj, gate_hid, wa2, ba2, wo
         x_pool = ctx.enter_context(tc.tile_pool(name="x", bufs=4))
         prod_pool = ctx.enter_context(tc.tile_pool(name="prod", bufs=3))
         quant_pool = ctx.enter_context(tc.tile_pool(name="quant", bufs=3))
-        out_pool = ctx.enter_context(tc.tile_pool(name="outs", bufs=4))
+        out_pool = ctx.enter_context(tc.tile_pool(name="outs", bufs=5))
         psum_gate = ctx.enter_context(tc.psum_pool(name="psum_gate", bufs=1))
         psum_sum = ctx.enter_context(tc.psum_pool(name="psum_sum", bufs=4))
         psum_out = ctx.enter_context(tc.psum_pool(name="psum_out", bufs=2))
@@ -75,6 +72,7 @@ def tile_hiremodule_pc_t_kernel(tc, h_mix, w_mix, c_proj, gate_hid, wa2, ba2, wo
         gate = [const.tile([P, C], F32, name="gate%d" % k) for k in range(STREAMS)]
         top = const.tile([P, C], F32, name="top")
         total = const.tile([P, C], F32, name="total")
+        token = const.tile([P, 1], F32, name="token")
         gate_flipped = [const.tile([P, PACK, P], F32, name="gate_flipped%d" % k) for k in range(2)]
 
         nc.vector.memset(ones[:], 1.0)
@@ -154,7 +152,7 @@ def tile_hiremodule_pc_t_kernel(tc, h_mix, w_mix, c_proj, gate_hid, wa2, ba2, wo
         nc.vector.tensor_tensor(out=total[:], in0=gate[2][:], in1=gate[0][:], op=ALU.add)
         nc.vector.tensor_tensor(out=total[:], in0=total[:], in1=gate[1][:], op=ALU.add)
         nc.vector.reciprocal(out=total[:], in_=total[:])
-        for k in (2, 0, 1):
+        for k in range(STREAMS):
             nc.vector.tensor_tensor(out=gate[k][:], in0=gate[k][:], in1=total[:], op=ALU.mult)
         nc.scalar.copy(out=bo_all[:], in_=bo_psum[:])
 
@@ -180,14 +178,15 @@ def tile_hiremodule_pc_t_kernel(tc, h_mix, w_mix, c_proj, gate_hid, wa2, ba2, wo
         out_tiles = {}
         flipped_tiles = {}
 
-        def multiply(engine, k, group, a_k, tag, bufs, at_once=GROUP):
-            start, count = span(group, GROUP)
+        def multiply(engine, k, start, count, a_k, tag, bufs, at_once):
+            product = prod_pool.tile(
+                [P, PACK, count, P], F32, name="%s_%d" % (tag, start), tag=tag, bufs=bufs, align_bytes=64
+            )
             for first in range(start, start + count, at_once):
                 n = min(at_once, start + count - first)
                 chunk = first // CHUNK
-                product = prod_pool.tile([P, PACK, n, P], F32, name="%s_%d" % (tag, first), tag=tag, bufs=bufs * GROUP // at_once)
                 engine.tensor_tensor(
-                    out=product[:].rearrange("b t j (s r) -> b t j s r", r=RUN),
+                    out=product[:, :, first - start : first - start + n, :].rearrange("b t j (s r) -> b t j s r", r=RUN),
                     in0=x_tiles[(k, chunk)][:, first % CHUNK : first % CHUNK + n, :].rearrange(
                         "b j (s t r) -> b t j s r", t=PACK, r=RUN
                     ),
@@ -198,17 +197,16 @@ def tile_hiremodule_pc_t_kernel(tc, h_mix, w_mix, c_proj, gate_hid, wa2, ba2, wo
                     op=ALU.mult,
                 )
                 for j in range(n):
-                    products[(k, first + j)] = (product, j)
+                    products[(k, first + j)] = (product, first - start + j)
 
         def vector_products(group, a):
-            multiply(nc.vector, 0, group, a[0], "vector0", 3)
-            if not w_on_gpsimd(group):
-                multiply(nc.vector, 1, group, a[1], "vector1", 3)
+            first, n = span(group, GROUP)
+            multiply(nc.vector, 0, first, n, a[0], "vector0", 3, n)
+            multiply(nc.vector, 1, first, n, a[1], "vector1", 3, n)
 
-        def gpsimd_products(group):
-            if w_on_gpsimd(group):
-                multiply(nc.gpsimd, 1, group, gate[1], "gpsimd1", 3)
-            multiply(nc.gpsimd, 2, group, gate[2], "gpsimd2", 4)
+        def gpsimd_products(batch, at_once):
+            first, n = span(batch, BATCH)
+            multiply(nc.gpsimd, 2, first, n, gate[2], "gpsimd2", 3, at_once)
 
         def sum_transposed(group):
             first, n = span(group, GROUP)
@@ -310,50 +308,62 @@ def tile_hiremodule_pc_t_kernel(tc, h_mix, w_mix, c_proj, gate_hid, wa2, ba2, wo
             first, n = span(group, GROUP)
             nc.scalar.dma_start(out=out_rows[:, first : first + n, :], in_=out_tiles[group][:, 0:n, :])
 
-        gpsimd_products(0)
-        gpsimd_products(1)
-        vector_products(0, gate)
+        nc.vector.tensor_copy(out=token[:], in_=gate[2][:, 0:1])
+        multiply(nc.vector, 2, 0, GROUP, gate[2], "vector0", 3, GROUP)
         nc.vector.quantize_mx(
             out=wo_codes[:].bitcast(FP8X4),
             scales=wo_scales[:],
             in_=wo_grouped[:].rearrange("p n t -> p (n t)"),
         )
+        multiply(nc.gpsimd, 2, GROUP, GROUP, gate[2], "gpsimd2", 3, GROUP)
+        gpsimd_products(1, BATCH)
+        gpsimd_products(2, BATCH)
+        vector_products(0, gate_psum)
 
         for step in range(n_groups):
-            if step % 2 == 0 and step >= 4:
-                quantise(step // 2 - 2)
-            if step >= 5 and not is_flipped((step - 5) // 2):
-                add_bias(step - 5)
-                store(step - 5)
+            batch = (step - 5) // 2
+            if step % 2 == 1 and batch >= 0:
+                if batch + 3 < n_batches:
+                    nc.vector.tensor_copy(out=gate[2][:, 0:1], in_=token[:])
+                quantise(batch)
+            if step >= 6 and not is_flipped((step - 6) // 2):
+                add_bias(step - 6)
+                store(step - 6)
             if step >= 1:
                 vector_products(step, gate_psum)
-            if step + 2 < n_groups:
-                gpsimd_products(step + 2)
+            if step % 2 == 1 and batch >= 0 and batch + 3 < n_batches:
+                gpsimd_products(batch + 3, BATCH)
             if step % 4 == 3 and step // 4 + 4 < n_chunks:
                 load_chunk(step // 4 + 4)
             if step >= 1:
                 sum_transposed(step - 1)
+            if step >= 5:
+                if is_flipped((step - 5) // 2):
+                    project_flipped((step - 5) // 2, range(2) if step % 2 == 1 else range(2, PACK))
+                else:
+                    project(step - 5)
             if step >= 7 and is_flipped((step - 7) // 2):
                 unflip(step - 7)
                 store(step - 7)
-            if step >= 4:
-                if is_flipped((step - 4) // 2):
-                    project_flipped((step - 4) // 2, range(2) if step % 2 == 0 else range(2, PACK))
-                else:
-                    project(step - 4)
 
         last = n_groups - 1
+        quantise(n_batches - 3)
         sum_transposed(last)
+        add_bias(last - 5)
+        store(last - 5)
+        project(last - 4)
+        project(last - 3, psum_sum, "f")
+        quantise(n_batches - 2)
         add_bias(last - 4)
         store(last - 4)
-        quantise(n_batches - 2)
-        project(last - 3)
-        project(last - 2, psum_sum, "f")
+        project(last - 2)
+        project(last - 1, psum_sum, "f")
         add_bias(last - 3)
         store(last - 3)
         quantise(n_batches - 1)
-        project(last - 1)
-        project(last, psum_sum, "f")
-        for group in range(last - 2, n_groups):
+        add_bias(last - 2)
+        store(last - 2)
+        project(last)
+        for group in (last - 1, last):
             add_bias(group)
             store(group)

@@ -76,7 +76,13 @@ def tile_hiremodule_pc_t_kernel(tc, h_mix, w_mix, c_proj, gate_hid, wa2, ba2, wo
         gate_flipped = [const.tile([P, PACK, P], F32, name="gate_flipped%d" % k) for k in range(2)]
 
         nc.vector.memset(ones[:], 1.0)
-        nc.gpsimd.memset(bias_rows[:].bitcast(I32), 0)
+        nc.gpsimd.memset(bias_rows[:, 0 : STREAMS * C // 2].bitcast(I32), 0)
+        nc.vector.memset(bias_rows[:, STREAMS * C // 2 : STREAMS * C].bitcast(I32), 0)
+        for k in range(STREAMS):
+            nc.scalar.dma_start(
+                out=bias_rows[32 * k : 32 * k + 1, 0 : STREAMS * C - 2],
+                in_=ba2.unsqueeze(0)[:, k : STREAMS * C - 2 + k],
+            )
         for k in (1, 2):
             nc.vector.memset(pick[k - 1][:].bitcast(I32), 0)
             nc.vector.memset(pick[k - 1][0:1, :], -1.0)
@@ -88,17 +94,14 @@ def tile_hiremodule_pc_t_kernel(tc, h_mix, w_mix, c_proj, gate_hid, wa2, ba2, wo
 
         nc.sync.dma_start(out=gate_sb[:], in_=gate_hid)
         nc.sync.dma_start(out=wa2_sb[:], in_=wa2)
-        for k in range(STREAMS):
-            nc.sync.dma_start(
-                out=bias_rows[32 * k : 32 * k + 1, 0 : STREAMS * C - 2],
-                in_=ba2.unsqueeze(0)[:, k : STREAMS * C - 2 + k],
-            )
-        nc.sync.dma_start(out=bias_rows[0:1, STREAMS * C :], in_=bo.unsqueeze(0))
+        nc.gpsimd.memset(bias_rows[:, STREAMS * C :].bitcast(I32), 0)
         for s in range(BLOCKS):
             nc.sync.dma_start(
                 out=wo_rows[s * RUN : (s + 1) * RUN, :, :],
                 in_=wo[s * PACK * RUN : (s + 1) * PACK * RUN, :].rearrange("(t r) n -> r t n", t=PACK),
             )
+
+        nc.sync.dma_start(out=bias_rows[0:1, STREAMS * C :], in_=bo.unsqueeze(0))
 
         x_tiles = {}
 
@@ -128,7 +131,7 @@ def tile_hiremodule_pc_t_kernel(tc, h_mix, w_mix, c_proj, gate_hid, wa2, ba2, wo
         flipped = psum_out.tile([P, P], BF16, name="flipped", tag="o")
         nc.tensor.transpose(flipped[:], gate_sb[:], ident_bf16[:])
         nc.vector.tensor_copy(out=gate_t[:], in_=flipped[:])
-        nc.scalar.mul(out=minus_gate_t[:], in_=flipped[:], mul=-1.0)
+        nc.vector.tensor_scalar(out=minus_gate_t[:], in0=flipped[:], scalar1=-1.0, scalar2=None, op0=ALU.mult)
 
         ba2_by_stream = bias_rows[:, 0 : STREAMS * C].rearrange("g (s t r k) -> g k t s r", t=PACK, r=RUN, k=STREAMS)
         wa2_by_stream = wa2_sb[:].rearrange("g (s t r k) -> g k t s r", t=PACK, r=RUN, k=STREAMS)
@@ -140,20 +143,31 @@ def tile_hiremodule_pc_t_kernel(tc, h_mix, w_mix, c_proj, gate_hid, wa2, ba2, wo
         bo_psum = psum_out.tile([P, C], F32, name="bo_psum", tag="o")
         nc.tensor.matmul(bo_psum[:], lhsT=ones[:], rhs=bias_rows[:, STREAMS * C :], start=True, stop=True)
 
-        nc.scalar.copy(out=gate[1][:], in_=diff[1][:])
-        nc.vector.scalar_tensor_tensor(
-            out=top[:], in0=diff[2][:], scalar=0.0, in1=gate[1][:], op0=ALU.max, op1=ALU.max
+        nc.scalar.activation(out=gate[1][:], in_=diff[1][:], func=ACT.Tanh, scale=0.5)
+        nc.scalar.activation(out=top[:], in_=diff[1][:], func=ACT.Abs)
+        nc.scalar.activation(out=top[:], in_=top[:], func=ACT.Exp, scale=-1.0)
+        nc.scalar.activation(out=top[:], in_=top[:], func=ACT.Ln, bias=1.0)
+        nc.vector.tensor_scalar(
+            out=gate[1][:], in0=gate[1][:], scalar1=0.5, scalar2=0.5, op0=ALU.mult, op1=ALU.add
         )
-        nc.scalar.activation(out=gate[0][:], in_=top[:], func=ACT.Exp, scale=-1.0)
+        nc.vector.scalar_tensor_tensor(
+            out=top[:], in0=diff[1][:], scalar=0.0, in1=top[:], op0=ALU.max, op1=ALU.add
+        )
         nc.vector.tensor_tensor(out=gate[2][:], in0=diff[2][:], in1=top[:], op=ALU.subtract)
-        nc.scalar.activation(out=gate[2][:], in_=gate[2][:], func=ACT.Exp)
-        nc.vector.tensor_tensor(out=gate[1][:], in0=diff[1][:], in1=top[:], op=ALU.subtract)
-        nc.scalar.activation(out=gate[1][:], in_=gate[1][:], func=ACT.Exp)
-        nc.vector.tensor_tensor(out=total[:], in0=gate[2][:], in1=gate[0][:], op=ALU.add)
-        nc.vector.tensor_tensor(out=total[:], in0=total[:], in1=gate[1][:], op=ALU.add)
-        nc.vector.reciprocal(out=total[:], in_=total[:])
-        for k in range(STREAMS):
-            nc.vector.tensor_tensor(out=gate[k][:], in0=gate[k][:], in1=total[:], op=ALU.mult)
+        nc.scalar.activation(out=gate[2][:], in_=gate[2][:], func=ACT.Tanh, scale=0.5)
+        nc.vector.quantize_mx(
+            out=wo_codes[:].bitcast(FP8X4),
+            scales=wo_scales[:],
+            in_=wo_grouped[:].rearrange("p n t -> p (n t)"),
+        )
+        nc.vector.tensor_scalar(
+            out=total[:], in0=gate[2][:], scalar1=-0.5, scalar2=0.5, op0=ALU.mult, op1=ALU.add
+        )
+        nc.vector.tensor_tensor(out=gate[1][:], in0=gate[1][:], in1=total[:], op=ALU.mult)
+        nc.vector.tensor_tensor(out=gate[0][:], in0=total[:], in1=gate[1][:], op=ALU.subtract)
+        nc.vector.tensor_scalar(
+            out=gate[2][:], in0=gate[2][:], scalar1=0.5, scalar2=0.5, op0=ALU.mult, op1=ALU.add
+        )
         nc.scalar.copy(out=bo_all[:], in_=bo_psum[:])
 
         gate_psum = [psum_gate.tile([P, C], F32, name="gate_psum%d" % k, tag="a%d" % k) for k in range(2)]
@@ -310,11 +324,6 @@ def tile_hiremodule_pc_t_kernel(tc, h_mix, w_mix, c_proj, gate_hid, wa2, ba2, wo
 
         nc.vector.tensor_copy(out=token[:], in_=gate[2][:, 0:1])
         multiply(nc.vector, 2, 0, GROUP, gate[2], "vector0", 3, GROUP)
-        nc.vector.quantize_mx(
-            out=wo_codes[:].bitcast(FP8X4),
-            scales=wo_scales[:],
-            in_=wo_grouped[:].rearrange("p n t -> p (n t)"),
-        )
         multiply(nc.gpsimd, 2, GROUP, GROUP, gate[2], "gpsimd2", 3, GROUP)
         gpsimd_products(1, BATCH)
         gpsimd_products(2, BATCH)

@@ -45,10 +45,10 @@ def tile_hiremodule_pc_t_kernel(tc, h_mix, w_mix, c_proj, gate_hid, wa2, ba2, wo
     with ExitStack() as ctx:
         ctx.enter_context(tc.manual_schedule())
         const = ctx.enter_context(tc.tile_pool(name="const", bufs=1))
-        x_pool = ctx.enter_context(tc.tile_pool(name="x", bufs=4))
+        x_pool = ctx.enter_context(tc.tile_pool(name="x", bufs=3))
         prod_pool = ctx.enter_context(tc.tile_pool(name="prod", bufs=3))
         quant_pool = ctx.enter_context(tc.tile_pool(name="quant", bufs=3))
-        out_pool = ctx.enter_context(tc.tile_pool(name="outs", bufs=5))
+        out_pool = ctx.enter_context(tc.tile_pool(name="outs", bufs=8))
         psum_gate = ctx.enter_context(tc.psum_pool(name="psum_gate", bufs=1))
         psum_sum = ctx.enter_context(tc.psum_pool(name="psum_sum", bufs=4))
         psum_out = ctx.enter_context(tc.psum_pool(name="psum_out", bufs=2))
@@ -88,7 +88,7 @@ def tile_hiremodule_pc_t_kernel(tc, h_mix, w_mix, c_proj, gate_hid, wa2, ba2, wo
             nc.vector.memset(pick[k - 1][0:1, :], -1.0)
             nc.vector.memset(pick[k - 1][32 * k : 32 * k + 1, :], 1.0)
         nc.vector.memset(warm[:, 0:1], 0.0)
-        nc.scalar.activation(out=warm[:, 1:2], in_=warm[:, 0:1], func=ACT.Exp)
+        nc.scalar.activation(out=warm[:, 1:2], in_=warm[:, 0:1], func=ACT.Tanh)
         make_identity(nc, ident_bf16[:])
         make_identity(nc, ident_f32[:])
 
@@ -107,12 +107,12 @@ def tile_hiremodule_pc_t_kernel(tc, h_mix, w_mix, c_proj, gate_hid, wa2, ba2, wo
 
         def load_chunk(chunk):
             first, n = span(chunk, CHUNK)
-            for k in range(STREAMS):
+            for k in reversed(range(STREAMS)):
                 x = x_pool.tile([P, n, C], BF16, name="x%d_%d" % (k, chunk), tag="x%d" % k)
                 nc.sync.dma_start(out=x[:], in_=streams[k][:, first : first + n, :])
                 x_tiles[(k, chunk)] = x
 
-        for chunk in range(4):
+        for chunk in range(3):
             load_chunk(chunk)
 
         nc.gpsimd.tensor_scalar(
@@ -144,39 +144,43 @@ def tile_hiremodule_pc_t_kernel(tc, h_mix, w_mix, c_proj, gate_hid, wa2, ba2, wo
         nc.tensor.matmul(bo_psum[:], lhsT=ones[:], rhs=bias_rows[:, STREAMS * C :], start=True, stop=True)
 
         nc.scalar.activation(out=gate[1][:], in_=diff[1][:], func=ACT.Tanh, scale=0.5)
-        nc.scalar.activation(out=top[:], in_=diff[1][:], func=ACT.Abs)
-        nc.scalar.activation(out=top[:], in_=top[:], func=ACT.Exp, scale=-1.0)
-        nc.scalar.activation(out=top[:], in_=top[:], func=ACT.Ln, bias=1.0)
+        nc.vector.scalar_tensor_tensor(
+            out=top[:], in0=gate[1][:], scalar=-1.0, in1=gate[1][:], op0=ALU.mult, op1=ALU.max
+        )
+        nc.scalar.activation(out=top[:], in_=top[:], func=ACT.Ln, scale=0.5, bias=0.5)
+        nc.vector.tensor_scalar(
+            out=gate[0][:], in0=gate[1][:], scalar1=-0.5, scalar2=0.5, op0=ALU.mult, op1=ALU.add
+        )
         nc.vector.tensor_scalar(
             out=gate[1][:], in0=gate[1][:], scalar1=0.5, scalar2=0.5, op0=ALU.mult, op1=ALU.add
         )
         nc.vector.scalar_tensor_tensor(
-            out=top[:], in0=diff[1][:], scalar=0.0, in1=top[:], op0=ALU.max, op1=ALU.add
+            out=top[:], in0=diff[1][:], scalar=0.0, in1=top[:], op0=ALU.max, op1=ALU.subtract
         )
         nc.vector.tensor_tensor(out=gate[2][:], in0=diff[2][:], in1=top[:], op=ALU.subtract)
         nc.scalar.activation(out=gate[2][:], in_=gate[2][:], func=ACT.Tanh, scale=0.5)
+        nc.vector.tensor_scalar(
+            out=total[:], in0=gate[2][:], scalar1=-0.5, scalar2=0.5, op0=ALU.mult, op1=ALU.add
+        )
+        for k in (1, 0):
+            nc.vector.tensor_tensor(out=gate[k][:], in0=gate[k][:], in1=total[:], op=ALU.mult)
         nc.vector.quantize_mx(
             out=wo_codes[:].bitcast(FP8X4),
             scales=wo_scales[:],
             in_=wo_grouped[:].rearrange("p n t -> p (n t)"),
         )
         nc.vector.tensor_scalar(
-            out=total[:], in0=gate[2][:], scalar1=-0.5, scalar2=0.5, op0=ALU.mult, op1=ALU.add
-        )
-        nc.vector.tensor_tensor(out=gate[1][:], in0=gate[1][:], in1=total[:], op=ALU.mult)
-        nc.vector.tensor_tensor(out=gate[0][:], in0=total[:], in1=gate[1][:], op=ALU.subtract)
-        nc.vector.tensor_scalar(
             out=gate[2][:], in0=gate[2][:], scalar1=0.5, scalar2=0.5, op0=ALU.mult, op1=ALU.add
         )
         nc.scalar.copy(out=bo_all[:], in_=bo_psum[:])
 
         gate_psum = [psum_gate.tile([P, C], F32, name="gate_psum%d" % k, tag="a%d" % k) for k in range(2)]
-        for k in range(2):
+        for k in (1, 0):
             turned = psum_sum.tile([P, PACK, P], F32, name="turned%d" % k, tag="f")
             for t in range(PACK):
                 nc.tensor.transpose(turned[:, t, :], gate[k][:, t * P : (t + 1) * P], ident_f32[:])
             nc.scalar.copy(out=gate_flipped[k][:], in_=turned[:])
-        for k in range(2):
+        for k in (1, 0):
             for t in range(PACK):
                 nc.tensor.transpose(gate_psum[k][:, t * P : (t + 1) * P], gate_flipped[k][:, t, :], ident_f32[:])
 
@@ -213,10 +217,9 @@ def tile_hiremodule_pc_t_kernel(tc, h_mix, w_mix, c_proj, gate_hid, wa2, ba2, wo
                 for j in range(n):
                     products[(k, first + j)] = (product, first - start + j)
 
-        def vector_products(group, a):
+        def vector_products(group, k):
             first, n = span(group, GROUP)
-            multiply(nc.vector, 0, first, n, a[0], "vector0", 3, n)
-            multiply(nc.vector, 1, first, n, a[1], "vector1", 3, n)
+            multiply(nc.vector, k, first, n, gate_psum[k], "vector%d" % k, 3, n)
 
         def gpsimd_products(batch, at_once):
             first, n = span(batch, BATCH)
@@ -322,12 +325,13 @@ def tile_hiremodule_pc_t_kernel(tc, h_mix, w_mix, c_proj, gate_hid, wa2, ba2, wo
             first, n = span(group, GROUP)
             nc.scalar.dma_start(out=out_rows[:, first : first + n, :], in_=out_tiles[group][:, 0:n, :])
 
-        nc.vector.tensor_copy(out=token[:], in_=gate[2][:, 0:1])
         multiply(nc.vector, 2, 0, GROUP, gate[2], "vector0", 3, GROUP)
+        nc.vector.tensor_copy(out=token[:], in_=gate[2][:, 0:1])
         multiply(nc.gpsimd, 2, GROUP, GROUP, gate[2], "gpsimd2", 3, GROUP)
         gpsimd_products(1, BATCH)
         gpsimd_products(2, BATCH)
-        vector_products(0, gate_psum)
+        for k in (1, 0):
+            vector_products(0, k)
 
         for step in range(n_groups):
             batch = (step - 5) // 2
@@ -339,11 +343,13 @@ def tile_hiremodule_pc_t_kernel(tc, h_mix, w_mix, c_proj, gate_hid, wa2, ba2, wo
                 add_bias(step - 6)
                 store(step - 6)
             if step >= 1:
-                vector_products(step, gate_psum)
+                vector_products(step, 0)
+            if step >= 1:
+                vector_products(step, 1)
             if step % 2 == 1 and batch >= 0 and batch + 3 < n_batches:
                 gpsimd_products(batch + 3, BATCH)
-            if step % 4 == 3 and step // 4 + 4 < n_chunks:
-                load_chunk(step // 4 + 4)
+            if step % 4 == 3 and step // 4 + 3 < n_chunks:
+                load_chunk(step // 4 + 3)
             if step >= 1:
                 sum_transposed(step - 1)
             if step >= 5:

@@ -75,11 +75,13 @@ def tile_hiremodule_pc_t_kernel(tc, h_mix, w_mix, c_proj, gate_hid, wa2, ba2, wo
         token = const.tile([P, 1], F32, name="token")
         gate_flipped = [const.tile([P, PACK, P], F32, name="gate_flipped%d" % k) for k in range(2)]
 
+        nc.sync.dma_start(out=gate_sb[:], in_=gate_hid)
+        nc.sync.dma_start(out=wa2_sb[:], in_=wa2)
         nc.vector.memset(ones[:], 1.0)
         nc.gpsimd.memset(bias_rows[:, 0 : STREAMS * C // 2].bitcast(I32), 0)
         nc.vector.memset(bias_rows[:, STREAMS * C // 2 : STREAMS * C].bitcast(I32), 0)
         for k in range(STREAMS):
-            nc.scalar.dma_start(
+            (nc.sync, nc.scalar, nc.scalar)[k].dma_start(
                 out=bias_rows[32 * k : 32 * k + 1, 0 : STREAMS * C - 2],
                 in_=ba2.unsqueeze(0)[:, k : STREAMS * C - 2 + k],
             )
@@ -92,8 +94,6 @@ def tile_hiremodule_pc_t_kernel(tc, h_mix, w_mix, c_proj, gate_hid, wa2, ba2, wo
         make_identity(nc, ident_bf16[:])
         make_identity(nc, ident_f32[:])
 
-        nc.sync.dma_start(out=gate_sb[:], in_=gate_hid)
-        nc.sync.dma_start(out=wa2_sb[:], in_=wa2)
         nc.gpsimd.memset(bias_rows[:, STREAMS * C :].bitcast(I32), 0)
         for s in range(BLOCKS):
             nc.sync.dma_start(
@@ -233,7 +233,7 @@ def tile_hiremodule_pc_t_kernel(tc, h_mix, w_mix, c_proj, gate_hid, wa2, ba2, wo
                     [P, BATCH, P, PACK], BF16, name="grouped%d" % batch, tag="grouped", align_bytes=64
                 )
             sums = [psum_sum.tile([P, PACK, P], F32, name="sum%d" % (first + j), tag="f") for j in range(n)]
-            for k in range(STREAMS):
+            for k in reversed(range(STREAMS)):
                 for j in range(n):
                     product, index = products[(k, first + j)]
                     for t in range(PACK):
@@ -242,8 +242,8 @@ def tile_hiremodule_pc_t_kernel(tc, h_mix, w_mix, c_proj, gate_hid, wa2, ba2, wo
                             lhsT=product[:, t, index, :],
                             rhs=ident_f32[:],
                             is_transpose=True,
-                            start=(k == 0 and t == 0),
-                            stop=(k == STREAMS - 1 and t == PACK - 1),
+                            start=(k == STREAMS - 1 and t == 0),
+                            stop=(k == 0 and t == PACK - 1),
                         )
             for j in range(n):
                 nc.scalar.copy(
@@ -343,9 +343,8 @@ def tile_hiremodule_pc_t_kernel(tc, h_mix, w_mix, c_proj, gate_hid, wa2, ba2, wo
                 add_bias(step - 6)
                 store(step - 6)
             if step >= 1:
-                vector_products(step, 0)
-            if step >= 1:
-                vector_products(step, 1)
+                for k in (1, 0):
+                    vector_products(step, k)
             if step % 2 == 1 and batch >= 0 and batch + 3 < n_batches:
                 gpsimd_products(batch + 3, BATCH)
             if step % 4 == 3 and step // 4 + 3 < n_chunks:

from contextlib import ExitStack

import concourse.mybir as mybir
from concourse.masks import make_identity

FLOPS = 2 * 128 * 49 * 512 * 512 + 2 * 128 * 128 * 1536

F32 = mybir.dt.float32
BF16 = mybir.dt.bfloat16
I32 = mybir.dt.int32
U32 = mybir.dt.uint32
U8 = mybir.dt.uint8
FP8X4 = mybir.dt.float8_e4m3fn_x4
ALU = mybir.AluOpType
ACT = mybir.ActivationFunctionType

P = 128
C = 512
PACK = 4
RUN = 8
BLOCKS = C // (PACK * RUN)
STREAMS = 3
POSITIONS = 49
GROUP = 2
BATCH = 4
CHUNK = 8
WARM_MATMULS = 12


def tile_hiremodule_pc_t_kernel(tc, h_mix, w_mix, c_proj, gate_hid, wa2, ba2, wo, bo, out):
    nc = tc.nc
    streams = [x.rearrange("b i j c -> b (i j) c") for x in (h_mix, w_mix, c_proj)]
    out_rows = out.rearrange("b i j c -> b (i j) c")

    n_chunks = (POSITIONS + CHUNK - 1) // CHUNK
    n_batches = (POSITIONS + BATCH - 1) // BATCH
    n_groups = (POSITIONS + GROUP - 1) // GROUP

    def span(index, size):
        return index * size, min(size, POSITIONS - index * size)

    def is_flipped(batch):
        return batch % 2 == 0 and batch < 9

    with ExitStack() as ctx:
        ctx.enter_context(tc.manual_schedule())
        const = ctx.enter_context(tc.tile_pool(name="const", bufs=1))
        x_pool = ctx.enter_context(tc.tile_pool(name="x", bufs=3))
        prod_pool = ctx.enter_context(tc.tile_pool(name="prod", bufs=3))
        quant_pool = ctx.enter_context(tc.tile_pool(name="quant", bufs=3))
        out_pool = ctx.enter_context(tc.tile_pool(name="outs", bufs=8))
        psum_gate = ctx.enter_context(tc.psum_pool(name="psum_gate", bufs=1))
        psum_sum = ctx.enter_context(tc.psum_pool(name="psum_sum", bufs=4))
        psum_out = ctx.enter_context(tc.psum_pool(name="psum_out", bufs=2))

        bias_rows = const.tile([P, STREAMS * C + C], BF16, name="bias_rows")
        ones = const.tile([P, P], BF16, name="ones")
        pick = [const.tile([P, P], BF16, name="pick%d" % k) for k in (1, 2)]
        warm = const.tile([P, 2], F32, name="warm")
        ident_bf16 = const.tile([P, P], BF16, name="ident_bf16")
        ident_f32 = const.tile([P, P], F32, name="ident_f32")
        gate_sb = const.tile([P, P], BF16, name="gate_sb")
        gate_t = const.tile([P, P], BF16, name="gate_t")
        minus_gate_t = const.tile([P, P], BF16, name="minus_gate_t")
        wa2_sb = const.tile([P, STREAMS * C], BF16, name="wa2_sb")
        wo_rows = const.tile([P, PACK, C], BF16, name="wo_rows")
        wo_grouped = const.tile([P, C, PACK], BF16, name="wo_grouped", align_bytes=64)
        wo_codes = const.tile([P, C], U32, name="wo_codes", align_bytes=64)
        wo_scales = const.tile([P, C], U8, name="wo_scales", align_bytes=64)
        bo_all = const.tile([P, C], F32, name="bo_all")
        bo_column = const.tile([P, PACK, 1], F32, name="bo_column")
        gate = [const.tile([P, C], F32, name="gate%d" % k) for k in range(STREAMS)]
        top = const.tile([P, C], F32, name="top")
        total = const.tile([P, C], F32, name="total")
        token = const.tile([P, 1], F32, name="token")
        gate_flipped = [const.tile([P, PACK, P], F32, name="gate_flipped%d" % k) for k in range(2)]

        nc.sync.dma_start(out=gate_sb[:], in_=gate_hid)
        nc.sync.dma_start(out=wa2_sb[:], in_=wa2)
        nc.vector.memset(ones[:], 1.0)
        nc.gpsimd.memset(bias_rows[:, 0 : STREAMS * C // 2].bitcast(I32), 0)
        nc.vector.memset(bias_rows[:, STREAMS * C // 2 : STREAMS * C].bitcast(I32), 0)
        for k in range(STREAMS):
            (nc.sync, nc.scalar, nc.scalar)[k].dma_start(
                out=bias_rows[32 * k : 32 * k + 1, 0 : STREAMS * C - 2],
                in_=ba2.unsqueeze(0)[:, k : STREAMS * C - 2 + k],
            )
        for k in (1, 2):
            nc.vector.memset(pick[k - 1][:].bitcast(I32), 0)
            nc.vector.memset(pick[k - 1][0:1, :], -1.0)
            nc.vector.memset(pick[k - 1][32 * k : 32 * k + 1, :], 1.0)
        nc.vector.memset(warm[:, 0:1], 0.0)
        nc.scalar.activation(out=warm[:, 1:2], in_=warm[:, 0:1], func=ACT.Tanh)
        make_identity(nc, ident_bf16[:])
        make_identity(nc, ident_f32[:])

        nc.gpsimd.memset(bias_rows[:, STREAMS * C :].bitcast(I32), 0)
        for s in range(BLOCKS):
            nc.sync.dma_start(
                out=wo_rows[s * RUN : (s + 1) * RUN, :, :],
                in_=wo[s * PACK * RUN : (s + 1) * PACK * RUN, :].rearrange("(t r) n -> r t n", t=PACK),
            )

        nc.sync.dma_start(out=bias_rows[0:1, STREAMS * C :], in_=bo.unsqueeze(0))

        x_tiles = {}

        def load_chunk(chunk):
            first, n = span(chunk, CHUNK)
            for k in reversed(range(STREAMS)):
                x = x_pool.tile([P, n, C], BF16, name="x%d_%d" % (k, chunk), tag="x%d" % k)
                nc.sync.dma_start(out=x[:], in_=streams[k][:, first : first + n, :])
                x_tiles[(k, chunk)] = x

        for chunk in range(3):
            load_chunk(chunk)

        nc.gpsimd.tensor_scalar(
            out=wo_grouped[:],
            in0=wo_rows[:].rearrange("p t n -> p n t"),
            scalar1=1.0,
            scalar2=0.0,
            op0=ALU.mult,
            op1=ALU.add,
        )

        spare = psum_out.tile([P, C], F32, name="spare", tag="o")
        for i in range(WARM_MATMULS):
            nc.tensor.matmul(spare[:, 0:P], lhsT=ones[:], rhs=ones[:], start=True, stop=True)

        flipped = psum_out.tile([P, P], BF16, name="flipped", tag="o")
        nc.tensor.transpose(flipped[:], gate_sb[:], ident_bf16[:])
        nc.vector.tensor_copy(out=gate_t[:], in_=flipped[:])
        nc.vector.tensor_scalar(out=minus_gate_t[:], in0=flipped[:], scalar1=-1.0, scalar2=None, op0=ALU.mult)

        ba2_by_stream = bias_rows[:, 0 : STREAMS * C].rearrange("g (s t r k) -> g k t s r", t=PACK, r=RUN, k=STREAMS)
        wa2_by_stream = wa2_sb[:].rearrange("g (s t r k) -> g k t s r", t=PACK, r=RUN, k=STREAMS)
        diff = {k: psum_sum.tile([P, C], F32, name="diff%d" % k, tag="f") for k in (1, 2)}
        for k in (1, 2):
            nc.tensor.matmul(diff[k][:], lhsT=gate_t[:], rhs=wa2_by_stream[:, k, :, :, :], start=True, stop=False)
            nc.tensor.matmul(diff[k][:], lhsT=minus_gate_t[:], rhs=wa2_by_stream[:, 0, :, :, :], start=False, stop=False)
            nc.tensor.matmul(diff[k][:], lhsT=pick[k - 1][:], rhs=ba2_by_stream[:, 0, :, :, :], start=False, stop=True)
        bo_psum = psum_out.tile([P, C], F32, name="bo_psum", tag="o")
        nc.tensor.matmul(bo_psum[:], lhsT=ones[:], rhs=bias_rows[:, STREAMS * C :], start=True, stop=True)

        nc.scalar.activation(out=gate[1][:], in_=diff[1][:], func=ACT.Tanh, scale=0.5)
        nc.vector.scalar_tensor_tensor(
            out=top[:], in0=gate[1][:], scalar=-1.0, in1=gate[1][:], op0=ALU.mult, op1=ALU.max
        )
        nc.scalar.activation(out=top[:], in_=top[:], func=ACT.Ln, scale=0.5, bias=0.5)
        nc.vector.tensor_scalar(
            out=gate[0][:], in0=gate[1][:], scalar1=-0.5, scalar2=0.5, op0=ALU.mult, op1=ALU.add
        )
        nc.vector.tensor_scalar(
            out=gate[1][:], in0=gate[1][:], scalar1=0.5, scalar2=0.5, op0=ALU.mult, op1=ALU.add
        )
        nc.vector.scalar_tensor_tensor(
            out=top[:], in0=diff[1][:], scalar=0.0, in1=top[:], op0=ALU.max, op1=ALU.subtract
        )
        nc.vector.tensor_tensor(out=gate[2][:], in0=diff[2][:], in1=top[:], op=ALU.subtract)
        nc.scalar.activation(out=gate[2][:], in_=gate[2][:], func=ACT.Tanh, scale=0.5)
        nc.vector.tensor_scalar(
            out=total[:], in0=gate[2][:], scalar1=-0.5, scalar2=0.5, op0=ALU.mult, op1=ALU.add
        )
        for k in (1, 0):
            nc.vector.tensor_tensor(out=gate[k][:], in0=gate[k][:], in1=total[:], op=ALU.mult)
        nc.vector.quantize_mx(
            out=wo_codes[:].bitcast(FP8X4),
            scales=wo_scales[:],
            in_=wo_grouped[:].rearrange("p n t -> p (n t)"),
        )
        nc.vector.tensor_scalar(
            out=gate[2][:], in0=gate[2][:], scalar1=0.5, scalar2=0.5, op0=ALU.mult, op1=ALU.add
        )
        nc.scalar.copy(out=bo_all[:], in_=bo_psum[:])

        gate_psum = [psum_gate.tile([P, C], F32, name="gate_psum%d" % k, tag="a%d" % k) for k in range(2)]
        for k in (1, 0):
            turned = psum_sum.tile([P, PACK, P], F32, name="turned%d" % k, tag="f")
            for t in range(PACK):
                nc.tensor.transpose(turned[:, t, :], gate[k][:, t * P : (t + 1) * P], ident_f32[:])
            nc.scalar.copy(out=gate_flipped[k][:], in_=turned[:])
        for k in (1, 0):
            for t in range(PACK):
                nc.tensor.transpose(gate_psum[k][:, t * P : (t + 1) * P], gate_flipped[k][:, t, :], ident_f32[:])

        turned = psum_sum.tile([P, PACK, P], F32, name="turned_bo", tag="f")
        for c in range(PACK):
            nc.tensor.transpose(turned[:, c, :], bo_all[:, c * P : (c + 1) * P], ident_f32[:])
        nc.scalar.copy(out=bo_column[:], in_=turned[:, :, 0:1])

        products = {}
        grouped_tiles = {}
        code_tiles = {}
        out_banks = {}
        out_tiles = {}
        flipped_tiles = {}

        def multiply(engine, k, start, count, a_k, tag, bufs, at_once):
            product = prod_pool.tile(
                [P, PACK, count, P], F32, name="%s_%d" % (tag, start), tag=tag, bufs=bufs, align_bytes=64
            )
            for first in range(start, start + count, at_once):
                n = min(at_once, start + count - first)
                chunk = first // CHUNK
                engine.tensor_tensor(
                    out=product[:, :, first - start : first - start + n, :].rearrange("b t j (s r) -> b t j s r", r=RUN),
                    in0=x_tiles[(k, chunk)][:, first % CHUNK : first % CHUNK + n, :].rearrange(
                        "b j (s t r) -> b t j s r", t=PACK, r=RUN
                    ),
                    in1=a_k[:]
                    .rearrange("b (t s r) -> b t s r", t=PACK, r=RUN)
                    .unsqueeze(2)
                    .to_broadcast([P, PACK, n, BLOCKS, RUN]),
                    op=ALU.mult,
                )
                for j in range(n):
                    products[(k, first + j)] = (product, first - start + j)

        def vector_products(group, k):
            first, n = span(group, GROUP)
            multiply(nc.vector, k, first, n, gate_psum[k], "vector%d" % k, 3, n)

        def gpsimd_products(batch, at_once):
            first, n = span(batch, BATCH)
            multiply(nc.gpsimd, 2, first, n, gate[2], "gpsimd2", 3, at_once)

        def sum_transposed(group):
            first, n = span(group, GROUP)
            batch = first // BATCH
            if first % BATCH == 0:
                grouped_tiles[batch] = quant_pool.tile(
                    [P, BATCH, P, PACK], BF16, name="grouped%d" % batch, tag="grouped", align_bytes=64
                )
            sums = [psum_sum.tile([P, PACK, P], F32, name="sum%d" % (first + j), tag="f") for j in range(n)]
            for k in reversed(range(STREAMS)):
                for j in range(n):
                    product, index = products[(k, first + j)]
                    for t in range(PACK):
                        nc.tensor.matmul(
                            sums[j][:, t, :],
                            lhsT=product[:, t, index, :],
                            rhs=ident_f32[:],
                            is_transpose=True,
                            start=(k == STREAMS - 1 and t == 0),
                            stop=(k == 0 and t == PACK - 1),
                        )
            for j in range(n):
                nc.scalar.copy(
                    out=grouped_tiles[batch][:, first % BATCH + j, :, :],
                    in_=sums[j][:].rearrange("p t b -> p b t"),
                )

        def quantise(batch):
            n = span(batch, BATCH)[1]
            codes = quant_pool.tile([P, BATCH * P], U32, name="codes%d" % batch, tag="codes", align_bytes=64)
            scales = quant_pool.tile([P, BATCH * P], U8, name="scales%d" % batch, tag="scales", align_bytes=64)
            code_tiles[batch] = (codes, scales)
            nc.vector.quantize_mx(
                out=codes[:, 0 : n * P].bitcast(FP8X4),
                scales=scales[:, 0 : n * P],
                in_=grouped_tiles[batch][:, 0:n, :, :].rearrange("p j b t -> p (j b t)"),
            )

        def project(group, pool=psum_out, tag="o"):
            first, n = span(group, GROUP)
            codes, scales = code_tiles[first // BATCH]
            for position in range(first, first + n):
                columns = slice((position % BATCH) * P, (position % BATCH + 1) * P)
                bank = pool.tile([P, C], F32, name="bank%d" % position, tag=tag)
                nc.tensor.matmul_mx(
                    out=bank[:],
                    lhsT=codes[:, columns].bitcast(FP8X4),
                    lhsT_scale=scales[:, columns],
                    rhs=wo_codes[:].bitcast(FP8X4),
                    rhs_scale=wo_scales[:],
                    start=True,
                    stop=True,
                )
                out_banks[position] = bank

        def project_flipped(batch, blocks):
            codes, scales = code_tiles[batch]
            if batch not in flipped_tiles:
                flipped_tiles[batch] = out_pool.tile(
                    [P, PACK, BATCH * P], F32, name="flipped%d" % batch, tag="flipped", bufs=2
                )
            for c in blocks:
                columns = slice(c * P, (c + 1) * P)
                bank = psum_out.tile([P, BATCH * P], F32, name="flip%d_%d" % (batch, c), tag="o")
                nc.tensor.matmul_mx(
                    out=bank[:],
                    lhsT=wo_codes[:, columns].bitcast(FP8X4),
                    lhsT_scale=wo_scales[:, columns],
                    rhs=codes[:].bitcast(FP8X4),
                    rhs_scale=scales[:],
                    start=True,
                    stop=True,
                )
                nc.scalar.activation(
                    out=flipped_tiles[batch][:, c, :], in_=bank[:], func=ACT.Identity, bias=bo_column[:, c, :]
                )

        def unflip(group):
            first, n = span(group, GROUP)
            out_tiles[group] = out_pool.tile([P, GROUP, C], F32, name="out%d" % group, tag="out")
            for j in range(n):
                columns = slice((first % BATCH + j) * P, (first % BATCH + j + 1) * P)
                bank = psum_sum.tile([P, C], F32, name="unflip%d" % (first + j), tag="f")
                for c in range(PACK):
                    nc.tensor.transpose(
                        bank[:, c * P : (c + 1) * P], flipped_tiles[first // BATCH][:, c, columns], ident_f32[:]
                    )
                nc.scalar.copy(out=out_tiles[group][:, j, :], in_=bank[:])

        def add_bias(group):
            first, n = span(group, GROUP)
            out_tiles[group] = out_pool.tile([P, GROUP, C], F32, name="out%d" % group, tag="out")
            for j in range(n):
                nc.vector.tensor_tensor(
                    out=out_tiles[group][:, j, :], in0=out_banks[first + j][:], in1=bo_all[:], op=ALU.add
                )

        def store(group):
            first, n = span(group, GROUP)
            nc.scalar.dma_start(out=out_rows[:, first : first + n, :], in_=out_tiles[group][:, 0:n, :])

        multiply(nc.vector, 2, 0, GROUP, gate[2], "vector0", 3, GROUP)
        nc.vector.tensor_copy(out=token[:], in_=gate[2][:, 0:1])
        multiply(nc.gpsimd, 2, GROUP, GROUP, gate[2], "gpsimd2", 3, GROUP)
        gpsimd_products(1, BATCH)
        gpsimd_products(2, BATCH)
        for k in (1, 0):
            vector_products(0, k)

        for step in range(n_groups):
            batch = (step - 5) // 2
            if step % 2 == 1 and batch >= 0:
                if batch + 3 < n_batches:
                    nc.vector.tensor_copy(out=gate[2][:, 0:1], in_=token[:])
                quantise(batch)
            if step >= 6 and not is_flipped((step - 6) // 2):
                add_bias(step - 6)
                store(step - 6)
            if step >= 1:
                for k in (1, 0):
                    vector_products(step, k)
            if step % 2 == 1 and batch >= 0 and batch + 3 < n_batches:
                gpsimd_products(batch + 3, BATCH)
            if step % 4 == 3 and step // 4 + 3 < n_chunks:
                load_chunk(step // 4 + 3)
            if step >= 1:
                sum_transposed(step - 1)
            if step >= 5:
                if is_flipped((step - 5) // 2):
                    project_flipped((step - 5) // 2, range(2) if step % 2 == 1 else range(2, PACK))
                else:
                    project(step - 5)
            if step >= 7 and is_flipped((step - 7) // 2):
                unflip(step - 7)
                store(step - 7)

        last = n_groups - 1
        quantise(n_batches - 3)
        sum_transposed(last)
        add_bias(last - 5)
        store(last - 5)
        project(last - 4)
        project(last - 3, psum_sum, "f")
        quantise(n_batches - 2)
        add_bias(last - 4)
        store(last - 4)
        project(last - 2)
        project(last - 1, psum_sum, "f")
        add_bias(last - 3)
        store(last - 3)
        quantise(n_batches - 1)
        add_bias(last - 2)
        store(last - 2)
        project(last)
        for group in (last - 1, last):
            add_bias(group)
            store(group)
